import numpy as np
import ml_dtypes


def mxq(x, axis, fmt="e4m3"):
    dtype, down = {"e4m3": (ml_dtypes.float8_e4m3fn, 7), "e5m2": (ml_dtypes.float8_e5m2, 14)}[fmt]
    v = np.moveaxis(np.asarray(x, np.float32).astype(ml_dtypes.bfloat16).astype(np.float64), axis, -1)
    blocks = v.reshape(v.shape[:-1] + (-1, 32))
    amax = np.abs(blocks).max(-1, keepdims=True)
    byte = np.maximum(np.where(amax > 0, np.frexp(amax)[1] - 1 + 127, 0) - down, 1)
    scale = np.exp2(byte - 127.0)
    codes = (blocks / scale).astype(np.float32).astype(dtype).astype(np.float64)
    return np.moveaxis((codes * scale).reshape(v.shape), -1, axis)


WIDE = False


def mx_kscale(k):
    if not WIDE:
        return np.ones(k)
    levels = np.array([10, -10, 5, -5, 0])
    if k % 512:
        return np.exp2(np.random.permutation(np.resize(levels, k // 32))).repeat(32)
    a = np.empty((k // 512, 16))
    for p in range(k // 512):
        a[p, :8] = np.random.permutation(np.resize(levels, 8))
        for g in range(8):
            far = levels[np.abs(levels - a[p, g]) >= 10]
            a[p, g + 8] = far[np.random.randint(len(far))]
    return np.exp2(a.ravel()).repeat(32)


BF16 = ml_dtypes.bfloat16


def bf(x):
    return np.asarray(x, np.float32).astype(BF16)


def f64(x):
    return np.asarray(x).astype(np.float64)


C, P, HWD, E, H, WS = 4, 8, 16, 2048, 16, 8
IMG = HWD * P
N = HWD * HWD * HWD
KC = C * P * P * P
G = HWD // WS
T = WS * WS
NW = N // T


def setup_inputs():
    r = np.random.standard_normal
    s = mx_kscale(KC).reshape(C, P, P, P)
    u = mx_kscale(E)
    sx = s[None, :, None, :, None, :, None, :]
    x = (r((1, C, HWD, P, HWD, P, HWD, P)) * sx).reshape(1, C, IMG, IMG, IMG)
    return {"x": bf(x),
            "conv_w": bf(r((E, C, P, P, P)) / np.sqrt(KC) / s * u[:, None, None, None, None]),
            "conv_b": bf(0.2 * r(E) * u),
            "emb_pos": bf(0.5 * r((N, E)) * u),
            "Wq": bf(0.5 * r((E, E)) / np.sqrt(E) / u), "bq": bf(0.1 * r(E)),
            "Wk": bf(0.5 * r((E, E)) / np.sqrt(E) / u), "bk": bf(0.1 * r(E)),
            "Wv": bf(3.0 * r((E, E)) / np.sqrt(E) / u), "bv": bf(0.5 * r(E))}


def reference(x, conv_w, conv_b, emb_pos, Wq, bq, Wk, bk, Wv, bv):
    xr = f64(x).reshape(1, C, HWD, P, HWD, P, HWD, P)
    patches = xr.transpose(0, 2, 4, 6, 1, 3, 5, 7).reshape(N, KC)
    wc = f64(conv_w).reshape(E, KC)
    t = (mxq(patches, 1, "e4m3") @ mxq(wc, 1, "e4m3").T) + f64(conv_b)
    t = t.reshape(1, N, E) + f64(emb_pos)
    v = t.reshape(1, G, WS, G, WS, G, WS, E)
    v = v.transpose(0, 1, 3, 5, 2, 4, 6, 7).reshape(NW, T, E)
    vq = mxq(v, 2, "e4m3")
    Q = (vq @ mxq(f64(Wq), 1, "e4m3").T) + f64(bq)
    K = (vq @ mxq(f64(Wk), 1, "e4m3").T) + f64(bk)
    V = (vq @ mxq(f64(Wv), 1, "e4m3").T) + f64(bv)
    return Q, K, V

@@ -1,0 +1,357 @@
+from contextlib import ExitStack
+
+import concourse.mybir as mybir
+from concourse.masks import make_identity
+
+FLOPS = 4 * 2 * 4096 * 2048 * 2048
+
+F32 = mybir.dt.float32
+BF16 = mybir.dt.bfloat16
+U32 = mybir.dt.uint32
+U8 = mybir.dt.uint8
+FP8X4 = mybir.dt.float8_e4m3fn_x4
+ADD = mybir.AluOpType.add
+
+P = 128
+KIB = 1024
+
+OFF_WC = 0
+OFF_WCP = 32 * KIB
+OFF_B = 34 * KIB
+OFF_BP = 66 * KIB
+OFF_C = 68 * KIB
+OFF_CP = 100 * KIB
+OFF_D = 102 * KIB
+OFF_DP = 134 * KIB
+OFF_XRAW = 136 * KIB
+OFF_WK = 152 * KIB
+OFF_WKP = 168 * KIB
+OFF_XS = 169 * KIB
+OFF_WRAW = 181 * KIB
+OFF_WS = 189 * KIB
+OFF_GRP = 197 * KIB
+OFF_EMB = 205 * KIB
+OFF_EC = 213 * KIB
+OFF_TS = 223 * KIB
+OFF_CB = 229 * KIB
+OFF_ID = 233 * KIB
+OFF_PERM = 233 * KIB + 512
+OFF_ST = 0
+
+
+def tile_swintransformerblock_pa_l_kernel(
+    tc, x, conv_w, conv_b, emb_pos, Wq, bq, Wk, bk, Wv, bv, out_0, out_1, out_2
+):
+    nc = tc.nc
+    with ExitStack() as ctx:
+        sb = ctx.enter_context(tc.tile_pool(name="sb", bufs=1))
+        ps = ctx.enter_context(tc.psum_pool(name="ps", bufs=4))
+        ctx.enter_context(tc.manual_schedule())
+
+        def sbuf(tag, shape, dtype, bufs, offset):
+            return sb.tile(shape, dtype, name=tag, tag=tag, bufs=bufs, offset=offset, align_bytes=64)
+
+        x_v = x.rearrange("b c (X i) (g w j) z -> (b c) i g X w (j z)", i=8, g=2, w=8, j=8)
+        emb_v = emb_pos.rearrange("(X g w z) e -> g z X w e", X=16, g=2, w=8, z=16)
+        wc_v = conv_w.rearrange("(G a q b h) c i j k -> G b a q h (c i j k)", G=4, a=2, q=64, b=2, h=2)
+        w_hbm = [Wq, Wk, Wv]
+        out_v = [
+            o.rearrange("s r o -> (s r) o").rearrange(
+                "(gx gy gz m wz) o -> gy gz wz m gx o", gx=2, gy=2, gz=2, m=64, wz=8
+            )
+            for o in (out_0, out_1, out_2)
+        ]
+
+        ident = sbuf("ident", [P, P], F32, 1, OFF_ID)
+        make_identity(nc, ident[:])
+        perm = sbuf("perm", [P, P], F32, 1, OFF_PERM)
+        nc.vector.tensor_copy(
+            out=perm[:].rearrange("p (m g) -> p g m", g=2), in_=ident[:].rearrange("p (g m) -> p g m", g=2)
+        )
+
+        wc_codes = sbuf("wc_codes", [P, 4, 2048], U32, 1, OFF_WC)
+        wc_plane = sbuf("wc_plane", [P, 2048], U8, 1, OFF_WCP)
+        x_codes = [sbuf("x0_codes", [P, 4, 2048], U32, 1, OFF_B), sbuf("x1_codes", [P, 4, 2048], U32, 1, OFF_C)]
+        x_plane = [sbuf("x0_plane", [P, 2048], U8, 1, OFF_BP), sbuf("x1_plane", [P, 2048], U8, 1, OFF_CP)]
+
+        pending = []
+
+        def drain(count):
+            for n in range(min(count, len(pending))):
+                grp, specs = pending.pop(0)
+                for lo, hi, codes, plane in specs:
+                    nc.vector.quantize_mx(out=codes.bitcast(FP8X4), scales=plane, in_=grp[:, lo:hi])
+
+        def run_banks(copy, banks):
+            tps = []
+            for sources, matrix, specs in banks:
+                tp = ps.tile([P, 512], F32, name="tp", tag="tp", bufs=4)
+                for n, src in enumerate(sources):
+                    nc.tensor.transpose(tp[:, n * P : (n + 1) * P], src, matrix[:])
+                tps.append(tp)
+            for tp, bank in zip(tps, banks):
+                grp = sbuf("grp", [P, 1024], BF16, 4, OFF_GRP)
+                copy(
+                    out=grp[:].bitcast(F32).rearrange("p (a r u) -> p a r u", a=2, u=2),
+                    in_=tp[:].rearrange("p (a u r) -> p a r u", a=2, u=2),
+                )
+                pending.append((grp, bank[2]))
+
+        x_raw = {}
+
+        def load_x_chunk(ci):
+            if ci >= 8:
+                return
+            u, c = divmod(ci, 4)
+            xr = sbuf("xraw", [P, 8, 1024], BF16, 2, OFF_XRAW)
+            for i in range(8):
+                nc.sync.dma_start(out=xr[:, i, :], in_=x_v[c, i, u])
+            x_raw[ci] = xr
+
+        def presort_x(copy, ci, zq):
+            xs = sbuf("xs", [P, 4, 2, P], F32, 3, OFF_XS)
+            src = (
+                x_raw[ci][:]
+                .rearrange("p i e -> p (i e)")
+                .bitcast(F32)
+                .rearrange("p (a z k u) -> p u z a k", a=64, z=16, k=2, u=2)
+            )
+            dst = xs[:].rearrange("p z u (a k) -> p u z a k", k=2)
+            for u in range(2):
+                copy(out=dst[:, u], in_=src[:, u, 4 * zq : 4 * zq + 4])
+            if zq == 3:
+                load_x_chunk(ci + 2)
+            return xs
+
+        def x_banks(xs, ci, zq):
+            u, c = divmod(ci, 4)
+            banks = []
+            for half in range(2):
+                z0 = 4 * zq + 2 * half
+                cols = (z0 * P, (z0 + 2) * P)
+                banks.append(
+                    (
+                        [xs[:, 2 * half + a, v, :] for a in range(2) for v in range(2)],
+                        ident,
+                        [(0, 1024, x_codes[u][:, c, cols[0] : cols[1]], x_plane[u][4 * c : P, cols[0] : cols[1]])],
+                    )
+                )
+            return banks
+
+        w_raw = {}
+
+        def load_w(key, rows):
+            wr = sbuf("wraw", [P, 2048], BF16, 2, OFF_WRAW)
+            nc.sync.dma_start(out=wr[:], in_=rows)
+            w_raw[key] = wr
+
+        def presort_w(copy, key):
+            ws = sbuf("ws", [P, 4, 2, P], F32, 2, OFF_WS)
+            copy(out=ws[:], in_=w_raw.pop(key)[:].bitcast(F32).rearrange("p (c m u) -> p c u m", c=4, u=2))
+            return ws
+
+        def w_banks(ws, codes, plane, col):
+            banks = []
+            for half in range(2):
+                banks.append(
+                    (
+                        [ws[:, 2 * half + a, v, :] for a in range(2) for v in range(2)],
+                        ident,
+                        [
+                            (
+                                512 * a,
+                                512 * (a + 1),
+                                codes[:, 2 * half + a, col : col + P],
+                                plane[4 * (2 * half + a) : P, col : col + P],
+                            )
+                            for a in range(2)
+                        ],
+                    )
+                )
+            return banks
+
+        def load_wc(k):
+            if k < 16:
+                G, blk = divmod(k, 4)
+                load_w(("wc", k), wc_v[G, blk // 2, blk % 2])
+
+        def load_wp(k):
+            if k < 48:
+                load_w(("wp", k), w_hbm[k // 16][(k % 16) * P : (k % 16 + 1) * P, :])
+
+        load_x_chunk(0)
+        load_wc(0)
+        load_wc(1)
+        load_x_chunk(1)
+        cb = sbuf("cb", [P, 2048], BF16, 1, OFF_CB)
+        nc.sync.dma_start(out=cb[:], in_=conv_b.partition_broadcast(P))
+
+        def head_presort(n):
+            if n % 2 == 0:
+                return presort_x(nc.vector.tensor_copy, n // 8, (n % 8) // 2)
+            ws = presort_w(nc.vector.tensor_copy, ("wc", n // 2))
+            load_wc(n // 2 + 2)
+            return ws
+
+        ems = {}
+
+        def load_emb(i):
+            if i < 32:
+                em = sbuf("emb", [P, 2048], BF16, 2, OFF_EMB)
+                nc.sync.dma_start(out=em[:], in_=emb_v[i // 16, i % 16])
+                ems[i] = em
+
+        sorted_next = head_presort(0)
+        for n in range(32):
+            sorted_now = sorted_next
+            if n + 1 < 32:
+                sorted_next = head_presort(n + 1)
+            if n == 24:
+                load_emb(0)
+                load_emb(1)
+            if n % 2 == 0:
+                banks = x_banks(sorted_now, n // 8, (n % 8) // 2)
+            else:
+                banks = w_banks(sorted_now, wc_codes, wc_plane, (n // 2) * P)
+            run_banks(nc.scalar.copy, banks)
+            if n > 0:
+                drain(2)
+
+        ecs = {}
+
+        def emb_plus_bias(i, G):
+            if i >= 32:
+                return
+            ec = sbuf("ec", [P, 512], F32, 5, OFF_EC)
+            eng = nc.vector if G % 2 == 0 else nc.gpsimd
+            eng.tensor_tensor(
+                out=ec[:].rearrange("q (u p h) -> q u p h", u=2, h=2),
+                in0=ems[i][:, G * 512 : (G + 1) * 512].rearrange("q (p u h) -> q u p h", u=2, h=2),
+                in1=cb[:, G * 512 : (G + 1) * 512].rearrange("q (p u h) -> q u p h", u=2, h=2),
+                op=ADD,
+            )
+            ecs[(i, G)] = ec
+
+        drain(2)
+        for G in range(4):
+            emb_plus_bias(0, G)
+
+        t_codes = [sbuf("t0_codes", [P, 4, 2048], U32, 1, OFF_D), None]
+        t_plane = [sbuf("t0_plane", [P, 2048], U8, 1, OFF_DP), None]
+        ts_tiles = {}
+        wk_tiles = {}
+        bias = []
+
+        def t_banks(i):
+            if i < 0:
+                return []
+            u, Z = divmod(i, 16)
+            banks = []
+            for gp in range(2):
+                words = ts_tiles.pop((i, gp))[:].bitcast(F32)
+                banks.append(
+                    (
+                        [words[:, n * P : (n + 1) * P] for n in range(4)],
+                        perm,
+                        [
+                            (
+                                512 * a,
+                                512 * (a + 1),
+                                t_codes[u][:, 2 * gp + a, Z * P : (Z + 1) * P],
+                                t_plane[u][4 * (2 * gp + a) : P, Z * P : (Z + 1) * P],
+                            )
+                            for a in range(2)
+                        ],
+                    )
+                )
+            return banks
+
+        def wp_presort(k):
+            ws = presort_w(nc.scalar.copy, ("wp", k))
+            load_wp(k + 2)
+            return ws
+
+        def wp_banks(ws, k):
+            j, blk = divmod(k, 4)
+            if blk == 0:
+                wk_tiles[j] = (
+                    sbuf("wk", [P, 4, 512], U32, 2, OFF_WK),
+                    sbuf("wkp", [P, 512], U8, 2, OFF_WKP),
+                )
+            return w_banks(ws, wk_tiles[j][0], wk_tiles[j][1], blk * P)
+
+        for i in range(32):
+            u, Z = divmod(i, 16)
+            load_emb(i + 2)
+            if i == 12:
+                load_wp(0)
+                load_wp(1)
+            if i == 16:
+                t_codes[1] = sbuf("t1_codes", [P, 4, 2048], U32, 1, OFF_B)
+                t_plane[1] = sbuf("t1_plane", [P, 2048], U8, 1, OFF_BP)
+            if i == 18:
+                for n, vec in enumerate((bq, bk, bv)):
+                    bt = sbuf("bias%d" % n, [P, 2048], BF16, 1, OFF_XS + n * 4 * KIB)
+                    nc.sync.dma_start(out=bt[:], in_=vec.partition_broadcast(P))
+                    bias.append(bt)
+            side = []
+            if u == 0:
+                side = x_banks(presort_x(nc.scalar.copy, 4 + i // 4, i % 4), 4 + i // 4, i % 4)
+            elif i % 2 == 0:
+                side = wp_banks(wp_presort((i - 16) // 2), (i - 16) // 2)
+            for G in range(4):
+                acc = ps.tile([P, 512], F32, name="mm", tag="mm", bufs=4)
+                for c in range(4):
+                    nc.tensor.matmul_mx(
+                        out=acc[:],
+                        lhsT=x_codes[u][:, c, Z * P : (Z + 1) * P].bitcast(FP8X4),
+                        lhsT_scale=x_plane[u][4 * c : P, Z * P : (Z + 1) * P],
+                        rhs=wc_codes[:, c, G * 512 : (G + 1) * 512].bitcast(FP8X4),
+                        rhs_scale=wc_plane[4 * c : P, G * 512 : (G + 1) * 512],
+                        start=(c == 0),
+                        stop=(c == 3),
+                    )
+                if G == 1:
+                    run_banks(nc.scalar.copy, t_banks(i - 1) + side)
+                if G % 2 == 0:
+                    ts_tiles[(i, G // 2)] = sbuf("ts", [P, 1024], BF16, 3, OFF_TS)
+                nc.vector.tensor_tensor(
+                    out=ts_tiles[(i, G // 2)][:, (G % 2) * 512 : (G % 2 + 1) * 512],
+                    in0=acc[:],
+                    in1=ecs.pop((i, G))[:],
+                    op=ADD,
+                )
+                emb_plus_bias(i + 1, G)
+                if G >= 2:
+                    drain(2)
+
+        sorted_w = []
+        for j in range(12):
+            wsel, oc = divmod(j, 4)
+            prep = 4 * (j + 1) if 2 <= j + 1 < 12 else None
+            for tau in range(32):
+                u, Z = divmod(tau, 16)
+                if prep is not None and tau in (2, 14):
+                    first = prep + (0 if tau == 2 else 2)
+                    sorted_w = [(wp_presort(first), first), (wp_presort(first + 1), first + 1)]
+                acc = ps.tile([P, 512], F32, name="mm", tag="mm", bufs=4)
+                for G in range(4):
+                    nc.tensor.matmul_mx(
+                        out=acc[:],
+                        lhsT=t_codes[u][:, G, Z * P : (Z + 1) * P].bitcast(FP8X4),
+                        lhsT_scale=t_plane[u][4 * G : P, Z * P : (Z + 1) * P],
+                        rhs=wk_tiles[j][0][:, G, :].bitcast(FP8X4),
+                        rhs_scale=wk_tiles[j][1][4 * G : P, :],
+                        start=(G == 0),
+                        stop=(G == 3),
+                    )
+                if j == 0 and tau == 1:
+                    run_banks(nc.scalar.copy, t_banks(31))
+                if prep is not None and tau in (6, 18):
+                    run_banks(nc.scalar.copy, wp_banks(sorted_w[0][0], sorted_w[0][1]) + wp_banks(sorted_w[1][0], sorted_w[1][1]))
+                st = sbuf("st", [P, 512], F32, 12, OFF_ST)
+                nc.vector.tensor_tensor(
+                    out=st[:], in0=acc[:], in1=bias[wsel][:, oc * 512 : (oc + 1) * 512], op=ADD
+                )
+                nc.sync.dma_start(out=out_v[wsel][u, Z // 8, Z % 8, :, :, oc * 512 : (oc + 1) * 512], in_=st[:])
+                drain(1)

@@ -29,13 +29,15 @@ OFF_WKP = 168 * KIB
 OFF_XS = 169 * KIB
 OFF_WRAW = 181 * KIB
 OFF_WS = 189 * KIB
-OFF_GRP = 197 * KIB
-OFF_EMB = 205 * KIB
-OFF_EC = 213 * KIB
-OFF_TS = 223 * KIB
-OFF_CB = 229 * KIB
+OFF_GRP = 201 * KIB
+OFF_ER = 209 * KIB
+OFF_EMBT = 217 * KIB
+OFF_TT = 225 * KIB
+OFF_GT = 229 * KIB
 OFF_ID = 233 * KIB
 OFF_PERM = 233 * KIB + 512
+OFF_CBB = 234 * KIB
+OFF_CBC = 234 * KIB + 64
 OFF_ST = 0
 
 
@@ -53,7 +55,7 @@ def tile_swintransformerblock_pa_l_kernel(
 
         x_v = x.rearrange("b c (X i) (g w j) z -> (b c) i g X w (j z)", i=8, g=2, w=8, j=8)
         emb_v = emb_pos.rearrange("(X g w z) e -> g z X w e", X=16, g=2, w=8, z=16)
-        wc_v = conv_w.rearrange("(G a q b h) c i j k -> G b a q h (c i j k)", G=4, a=2, q=64, b=2, h=2)
+        wc_v = conv_w.rearrange("(g m t) c i j k -> g t m (c i j k)", g=4, t=4)
         w_hbm = [Wq, Wk, Wv]
         out_v = [
             o.rearrange("s r o -> (s r) o").rearrange(
@@ -76,26 +78,32 @@ def tile_swintransformerblock_pa_l_kernel(
 
         pending = []
 
+        def quantize(grp, specs):
+            for lo, hi, codes, plane in specs:
+                nc.vector.quantize_mx(out=codes.bitcast(FP8X4), scales=plane, in_=grp[:, lo:hi])
+
         def drain(count):
             for n in range(min(count, len(pending))):
                 grp, specs = pending.pop(0)
-                for lo, hi, codes, plane in specs:
-                    nc.vector.quantize_mx(out=codes.bitcast(FP8X4), scales=plane, in_=grp[:, lo:hi])
+                quantize(grp, specs)
 
         def run_banks(copy, banks):
             tps = []
-            for sources, matrix, specs in banks:
+            for sources, matrix, dest, specs in banks:
                 tp = ps.tile([P, 512], F32, name="tp", tag="tp", bufs=4)
                 for n, src in enumerate(sources):
                     nc.tensor.transpose(tp[:, n * P : (n + 1) * P], src, matrix[:])
                 tps.append(tp)
             for tp, bank in zip(tps, banks):
-                grp = sbuf("grp", [P, 1024], BF16, 4, OFF_GRP)
-                copy(
-                    out=grp[:].bitcast(F32).rearrange("p (a r u) -> p a r u", a=2, u=2),
-                    in_=tp[:].rearrange("p (a u r) -> p a r u", a=2, u=2),
-                )
-                pending.append((grp, bank[2]))
+                if bank[2] is not None:
+                    copy(out=bank[2], in_=tp[:])
+                else:
+                    grp = sbuf("grp", [P, 1024], BF16, 4, OFF_GRP)
+                    copy(
+                        out=grp[:].bitcast(F32).rearrange("p (a r u) -> p a r u", a=2, u=2),
+                        in_=tp[:].rearrange("p (a u r) -> p a r u", a=2, u=2),
+                    )
+                    pending.append((grp, bank[3]))
 
         x_raw = {}
 
@@ -132,7 +140,8 @@ def tile_swintransformerblock_pa_l_kernel(
                 banks.append(
                     (
                         [xs[:, 2 * half + a, v, :] for a in range(2) for v in range(2)],
-                        ident,
+                        perm,
+                        None,
                         [(0, 1024, x_codes[u][:, c, cols[0] : cols[1]], x_plane[u][4 * c : P, cols[0] : cols[1]])],
                     )
                 )
@@ -146,7 +155,7 @@ def tile_swintransformerblock_pa_l_kernel(
             w_raw[key] = wr
 
         def presort_w(copy, key):
-            ws = sbuf("ws", [P, 4, 2, P], F32, 2, OFF_WS)
+            ws = sbuf("ws", [P, 4, 2, P], F32, 3, OFF_WS)
             copy(out=ws[:], in_=w_raw.pop(key)[:].bitcast(F32).rearrange("p (c m u) -> p c u m", c=4, u=2))
             return ws
 
@@ -157,6 +166,7 @@ def tile_swintransformerblock_pa_l_kernel(
                     (
                         [ws[:, 2 * half + a, v, :] for a in range(2) for v in range(2)],
                         ident,
+                        None,
                         [
                             (
                                 512 * a,
@@ -172,19 +182,54 @@ def tile_swintransformerblock_pa_l_kernel(
 
         def load_wc(k):
             if k < 16:
-                G, blk = divmod(k, 4)
-                load_w(("wc", k), wc_v[G, blk // 2, blk % 2])
+                load_w(("wc", k), wc_v[k // 4, k % 4])
 
         def load_wp(k):
             if k < 48:
                 load_w(("wp", k), w_hbm[k // 16][(k % 16) * P : (k % 16 + 1) * P, :])
 
+        er_tiles = {}
+        es_tiles = {}
+        emb_t = {}
+
+        def load_emb(s):
+            if s >= 32:
+                return
+            er = sbuf("er", [P, 4, 512], BF16, 2, OFF_ER)
+            for z in range(4):
+                nc.sync.dma_start(
+                    out=er[:, z, :],
+                    in_=emb_v[s // 16, 4 * ((s % 16) // 4) + z, :, :, (s % 4) * 512 : (s % 4 + 1) * 512],
+                )
+            er_tiles[s] = er
+
+        def presort_emb(copy, s):
+            if s >= 32:
+                return
+            es = sbuf("ws", [P, 4, 2, P], F32, 3, OFF_WS)
+            copy(
+                out=es[:],
+                in_=er_tiles.pop(s)[:]
+                .rearrange("p z e -> p (z e)")
+                .bitcast(F32)
+                .rearrange("p (z m v) -> p z v m", z=4, v=2),
+            )
+            es_tiles[s] = es
+
+        def emb_banks(s):
+            if s >= 32:
+                return []
+            es = es_tiles.pop(s)
+            et = sbuf("embt", [P, 2, 512], F32, 2, OFF_EMBT)
+            emb_t[s] = et
+            return [([es[:, z, v, :] for z in range(4)], perm, et[:, v, :], None) for v in range(2)]
+
+        cbb = sbuf("cbb", [P, 4, 4], BF16, 1, OFF_CBB)
+        nc.sync.dma_start(out=cbb[:], in_=conv_b.rearrange("(g p t) -> p g t", g=4, t=4))
         load_x_chunk(0)
         load_wc(0)
         load_wc(1)
         load_x_chunk(1)
-        cb = sbuf("cb", [P, 2048], BF16, 1, OFF_CB)
-        nc.sync.dma_start(out=cb[:], in_=conv_b.partition_broadcast(P))
 
         def head_presort(n):
             if n % 2 == 0:
@@ -193,20 +238,12 @@ def tile_swintransformerblock_pa_l_kernel(
             load_wc(n // 2 + 2)
             return ws
 
-        ems = {}
-
-        def load_emb(i):
-            if i < 32:
-                em = sbuf("emb", [P, 2048], BF16, 2, OFF_EMB)
-                nc.sync.dma_start(out=em[:], in_=emb_v[i // 16, i % 16])
-                ems[i] = em
-
         sorted_next = head_presort(0)
         for n in range(32):
             sorted_now = sorted_next
             if n + 1 < 32:
                 sorted_next = head_presort(n + 1)
-            if n == 24:
+            if n == 22:
                 load_emb(0)
                 load_emb(1)
             if n % 2 == 0:
@@ -217,54 +254,10 @@ def tile_swintransformerblock_pa_l_kernel(
             if n > 0:
                 drain(2)
 
-        ecs = {}
-
-        def emb_plus_bias(i, G):
-            if i >= 32:
-                return
-            ec = sbuf("ec", [P, 512], F32, 5, OFF_EC)
-            eng = nc.vector if G % 2 == 0 else nc.gpsimd
-            eng.tensor_tensor(
-                out=ec[:].rearrange("q (u p h) -> q u p h", u=2, h=2),
-                in0=ems[i][:, G * 512 : (G + 1) * 512].rearrange("q (p u h) -> q u p h", u=2, h=2),
-                in1=cb[:, G * 512 : (G + 1) * 512].rearrange("q (p u h) -> q u p h", u=2, h=2),
-                op=ADD,
-            )
-            ecs[(i, G)] = ec
-
-        drain(2)
-        for G in range(4):
-            emb_plus_bias(0, G)
-
         t_codes = [sbuf("t0_codes", [P, 4, 2048], U32, 1, OFF_D), None]
         t_plane = [sbuf("t0_plane", [P, 2048], U8, 1, OFF_DP), None]
-        ts_tiles = {}
         wk_tiles = {}
         bias = []
-
-        def t_banks(i):
-            if i < 0:
-                return []
-            u, Z = divmod(i, 16)
-            banks = []
-            for gp in range(2):
-                words = ts_tiles.pop((i, gp))[:].bitcast(F32)
-                banks.append(
-                    (
-                        [words[:, n * P : (n + 1) * P] for n in range(4)],
-                        perm,
-                        [
-                            (
-                                512 * a,
-                                512 * (a + 1),
-                                t_codes[u][:, 2 * gp + a, Z * P : (Z + 1) * P],
-                                t_plane[u][4 * (2 * gp + a) : P, Z * P : (Z + 1) * P],
-                            )
-                            for a in range(2)
-                        ],
-                    )
-                )
-            return banks
 
         def wp_presort(k):
             ws = presort_w(nc.scalar.copy, ("wp", k))
@@ -280,50 +273,90 @@ def tile_swintransformerblock_pa_l_kernel(
                 )
             return w_banks(ws, wk_tiles[j][0], wk_tiles[j][1], blk * P)
 
-        for i in range(32):
-            u, Z = divmod(i, 16)
-            load_emb(i + 2)
-            if i == 12:
+        def side_presort(s):
+            if s < 16:
+                return presort_x(nc.scalar.copy, 4 + s // 4, s % 4)
+            if s < 32 and s % 2 == 0:
+                return wp_presort((s - 16) // 2)
+            return None
+
+        def side_banks(s, thing):
+            if thing is None:
+                return []
+            if s < 16:
+                return x_banks(thing, 4 + s // 4, s % 4)
+            return wp_banks(thing, (s - 16) // 2)
+
+        cbc = sbuf("cbc", [P, 16], F32, 1, OFF_CBC)
+        nc.vector.tensor_copy(out=cbc[:], in_=cbb[:].rearrange("p g t -> p (g t)"))
+        presort_emb(nc.vector.tensor_copy, 0)
+        load_emb(2)
+        run_banks(nc.scalar.copy, emb_banks(0))
+        drain(2)
+        presort_emb(nc.vector.tensor_copy, 1)
+        side_next = side_presort(0)
+        t_waiting = []
+
+        for s in range(32):
+            u, zq, g = s // 16, (s % 16) // 4, s % 4
+            load_emb(s + 3)
+            if s == 11:
                 load_wp(0)
                 load_wp(1)
-            if i == 16:
+            if s == 16:
                 t_codes[1] = sbuf("t1_codes", [P, 4, 2048], U32, 1, OFF_B)
                 t_plane[1] = sbuf("t1_plane", [P, 2048], U8, 1, OFF_BP)
-            if i == 18:
+            if s == 18:
                 for n, vec in enumerate((bq, bk, bv)):
                     bt = sbuf("bias%d" % n, [P, 2048], BF16, 1, OFF_XS + n * 4 * KIB)
                     nc.sync.dma_start(out=bt[:], in_=vec.partition_broadcast(P))
                     bias.append(bt)
-            side = []
-            if u == 0:
-                side = x_banks(presort_x(nc.scalar.copy, 4 + i // 4, i % 4), 4 + i // 4, i % 4)
-            elif i % 2 == 0:
-                side = wp_banks(wp_presort((i - 16) // 2), (i - 16) // 2)
-            for G in range(4):
+            tt = sbuf("tt", [P, 4, 512], BF16, 1, OFF_TT)
+            et = emb_t.pop(s)
+            for t in range(4):
+                col = (4 * g + t) * P
                 acc = ps.tile([P, 512], F32, name="mm", tag="mm", bufs=4)
                 for c in range(4):
                     nc.tensor.matmul_mx(
                         out=acc[:],
-                        lhsT=x_codes[u][:, c, Z * P : (Z + 1) * P].bitcast(FP8X4),
-                        lhsT_scale=x_plane[u][4 * c : P, Z * P : (Z + 1) * P],
-                        rhs=wc_codes[:, c, G * 512 : (G + 1) * 512].bitcast(FP8X4),
-                        rhs_scale=wc_plane[4 * c : P, G * 512 : (G + 1) * 512],
+                        lhsT=wc_codes[:, c, col : col + P].bitcast(FP8X4),
+                        lhsT_scale=wc_plane[4 * c : P, col : col + P],
+                        rhs=x_codes[u][:, c, zq * 512 : (zq + 1) * 512].bitcast(FP8X4),
+                        rhs_scale=x_plane[u][4 * c : P, zq * 512 : (zq + 1) * 512],
                         start=(c == 0),
                         stop=(c == 3),
                     )
-                if G == 1:
-                    run_banks(nc.scalar.copy, t_banks(i - 1) + side)
-                if G % 2 == 0:
-                    ts_tiles[(i, G // 2)] = sbuf("ts", [P, 1024], BF16, 3, OFF_TS)
-                nc.vector.tensor_tensor(
-                    out=ts_tiles[(i, G // 2)][:, (G % 2) * 512 : (G % 2 + 1) * 512],
+                if t == 1:
+                    run_banks(nc.scalar.copy, emb_banks(s + 1) + side_banks(s, side_next))
+                    presort_emb(nc.scalar.copy, s + 2)
+                    side_next = side_presort(s + 1)
+                nc.vector.scalar_tensor_tensor(
+                    out=tt[:, t, :],
                     in0=acc[:],
-                    in1=ecs.pop((i, G))[:],
-                    op=ADD,
+                    scalar=cbc[:, 4 * g + t : 4 * g + t + 1],
+                    in1=et[:, t // 2, :].bitcast(BF16).rearrange("p (n h) -> p n h", h=2)[:, :, t % 2],
+                    op0=ADD,
+                    op1=ADD,
                 )
-                emb_plus_bias(i + 1, G)
-                if G >= 2:
-                    drain(2)
+                if t == 0 and len(t_waiting) > 0:
+                    gt_old, specs_old = t_waiting.pop(0)
+                    quantize(gt_old, specs_old)
+            gt = sbuf("gt", [P, 2048], BF16, 1, OFF_GT)
+            nc.vector.tensor_copy(out=gt[:].rearrange("p (n t) -> p n t", t=4), in_=tt[:].rearrange("p t n -> p n t"))
+            t_waiting.append(
+                (
+                    gt,
+                    [
+                        (
+                            0,
+                            2048,
+                            t_codes[u][:, g, zq * 512 : (zq + 1) * 512],
+                            t_plane[u][4 * g : P, zq * 512 : (zq + 1) * 512],
+                        )
+                    ],
+                )
+            )
+            drain(2)
 
         sorted_w = []
         for j in range(12):
@@ -345,13 +378,17 @@ def tile_swintransformerblock_pa_l_kernel(
                         start=(G == 0),
                         stop=(G == 3),
                     )
-                if j == 0 and tau == 1:
-                    run_banks(nc.scalar.copy, t_banks(31))
                 if prep is not None and tau in (6, 18):
-                    run_banks(nc.scalar.copy, wp_banks(sorted_w[0][0], sorted_w[0][1]) + wp_banks(sorted_w[1][0], sorted_w[1][1]))
+                    run_banks(
+                        nc.scalar.copy,
+                        wp_banks(sorted_w[0][0], sorted_w[0][1]) + wp_banks(sorted_w[1][0], sorted_w[1][1]),
+                    )
                 st = sbuf("st", [P, 512], F32, 12, OFF_ST)
                 nc.vector.tensor_tensor(
                     out=st[:], in0=acc[:], in1=bias[wsel][:, oc * 512 : (oc + 1) * 512], op=ADD
                 )
                 nc.sync.dma_start(out=out_v[wsel][u, Z // 8, Z % 8, :, :, oc * 512 : (oc + 1) * 512], in_=st[:])
+                if len(t_waiting) > 0:
+                    gt_old, specs_old = t_waiting.pop(0)
+                    quantize(gt_old, specs_old)
                 drain(1)

@@ -73,8 +73,8 @@ def tile_swintransformerblock_pa_l_kernel(
 
         wc_codes = sbuf("wc_codes", [P, 4, 2048], U32, 1, OFF_WC)
         wc_plane = sbuf("wc_plane", [P, 2048], U8, 1, OFF_WCP)
-        x_codes = [sbuf("x0_codes", [P, 4, 2048], U32, 1, OFF_B), sbuf("x1_codes", [P, 4, 2048], U32, 1, OFF_C)]
-        x_plane = [sbuf("x0_plane", [P, 2048], U8, 1, OFF_BP), sbuf("x1_plane", [P, 2048], U8, 1, OFF_CP)]
+        x_codes = [sbuf("x0_codes", [P, 4, 2048], U32, 1, OFF_B), None]
+        x_plane = [sbuf("x0_plane", [P, 2048], U8, 1, OFF_BP), None]
 
         pending = []
 
@@ -111,7 +111,10 @@ def tile_swintransformerblock_pa_l_kernel(
             if ci >= 8:
                 return
             u, c = divmod(ci, 4)
-            xr = sbuf("xraw", [P, 8, 1024], BF16, 2, OFF_XRAW)
+            if ci in (2, 3):
+                xr = sbuf("xrawd", [P, 8, 1024], BF16, 2, OFF_D)
+            else:
+                xr = sbuf("xraw", [P, 8, 1024], BF16, 2, OFF_XRAW)
             for i in range(8):
                 nc.sync.dma_start(out=xr[:, i, :], in_=x_v[c, i, u])
             x_raw[ci] = xr
@@ -127,7 +130,7 @@ def tile_swintransformerblock_pa_l_kernel(
             dst = xs[:].rearrange("p z u (a k) -> p u z a k", k=2)
             for u in range(2):
                 copy(out=dst[:, u], in_=src[:, u, 4 * zq : 4 * zq + 4])
-            if zq == 3:
+            if zq == 3 and ci >= 4:
                 load_x_chunk(ci + 2)
             return xs
 
@@ -182,7 +185,35 @@ def tile_swintransformerblock_pa_l_kernel(
 
         def load_wc(k):
             if k < 16:
-                load_w(("wc", k), wc_v[k // 4, k % 4])
+                wr = sbuf("wcraw", [P, 2048], BF16, 8, OFF_C)
+                nc.sync.dma_start(out=wr[:], in_=wc_v[k // 4, k % 4])
+                w_raw[("wc", k)] = wr
+
+        def wc_banks(k):
+            words = w_raw.pop(("wc", k))[:].bitcast(F32)
+            banks = []
+            for half in range(2):
+                banks.append(
+                    (
+                        [
+                            words[:, 256 * (2 * half + a) + v : 256 * (2 * half + a + 1) : 2]
+                            for a in range(2)
+                            for v in range(2)
+                        ],
+                        ident,
+                        None,
+                        [
+                            (
+                                512 * a,
+                                512 * (a + 1),
+                                wc_codes[:, 2 * half + a, k * P : (k + 1) * P],
+                                wc_plane[4 * (2 * half + a) : P, k * P : (k + 1) * P],
+                            )
+                            for a in range(2)
+                        ],
+                    )
+                )
+            return banks
 
         def load_wp(k):
             if k < 48:
@@ -227,33 +258,50 @@ def tile_swintransformerblock_pa_l_kernel(
         cbb = sbuf("cbb", [P, 4, 4], BF16, 1, OFF_CBB)
         nc.sync.dma_start(out=cbb[:], in_=conv_b.rearrange("(g p t) -> p g t", g=4, t=4))
         load_x_chunk(0)
-        load_wc(0)
-        load_wc(1)
+        for k in range(4):
+            load_wc(k)
         load_x_chunk(1)
+        for k in range(4, 8):
+            load_wc(k)
+        load_x_chunk(2)
 
         def head_presort(n):
             if n % 2 == 0:
                 return presort_x(nc.vector.tensor_copy, n // 8, (n % 8) // 2)
-            ws = presort_w(nc.vector.tensor_copy, ("wc", n // 2))
-            load_wc(n // 2 + 2)
-            return ws
+            return None
 
+        cbc = sbuf("cbc", [P, 16], F32, 1, OFF_CBC)
         sorted_next = head_presort(0)
         for n in range(32):
             sorted_now = sorted_next
             if n + 1 < 32:
                 sorted_next = head_presort(n + 1)
-            if n == 22:
-                load_emb(0)
-                load_emb(1)
             if n % 2 == 0:
                 banks = x_banks(sorted_now, n // 8, (n % 8) // 2)
             else:
-                banks = w_banks(sorted_now, wc_codes, wc_plane, (n // 2) * P)
+                banks = wc_banks(n // 2)
             run_banks(nc.scalar.copy, banks)
+            if n % 2 == 1:
+                load_wc(n // 2 + 8)
+            if n == 7:
+                load_x_chunk(3)
+            if n == 9:
+                load_emb(0)
+                load_emb(1)
+            if n == 20:
+                nc.vector.tensor_copy(out=cbc[:], in_=cbb[:].rearrange("p g t -> p (g t)"))
+            if n == 27:
+                presort_emb(nc.vector.tensor_copy, 0)
+                load_emb(2)
+            if n == 29:
+                run_banks(nc.scalar.copy, emb_banks(0))
+            if n == 30:
+                presort_emb(nc.vector.tensor_copy, 1)
             if n > 0:
                 drain(2)
 
+        x_codes[1] = sbuf("x1_codes", [P, 4, 2048], U32, 1, OFF_C)
+        x_plane[1] = sbuf("x1_plane", [P, 2048], U8, 1, OFF_CP)
         t_codes = [sbuf("t0_codes", [P, 4, 2048], U32, 1, OFF_D), None]
         t_plane = [sbuf("t0_plane", [P, 2048], U8, 1, OFF_DP), None]
         wk_tiles = {}
@@ -274,39 +322,36 @@ def tile_swintransformerblock_pa_l_kernel(
             return w_banks(ws, wk_tiles[j][0], wk_tiles[j][1], blk * P)
 
         def side_presort(s):
-            if s < 16:
-                return presort_x(nc.scalar.copy, 4 + s // 4, s % 4)
-            if s < 32 and s % 2 == 0:
-                return wp_presort((s - 16) // 2)
+            if 3 <= s < 19:
+                return presort_x(nc.scalar.copy, 4 + (s - 3) // 4, (s - 3) % 4)
+            if 24 <= s < 32:
+                return wp_presort(s - 24)
             return None
 
         def side_banks(s, thing):
             if thing is None:
                 return []
-            if s < 16:
-                return x_banks(thing, 4 + s // 4, s % 4)
-            return wp_banks(thing, (s - 16) // 2)
+            if s < 19:
+                return x_banks(thing, 4 + (s - 3) // 4, (s - 3) % 4)
+            return wp_banks(thing, s - 24)
 
-        cbc = sbuf("cbc", [P, 16], F32, 1, OFF_CBC)
-        nc.vector.tensor_copy(out=cbc[:], in_=cbb[:].rearrange("p g t -> p (g t)"))
-        presort_emb(nc.vector.tensor_copy, 0)
-        load_emb(2)
-        run_banks(nc.scalar.copy, emb_banks(0))
         drain(2)
-        presort_emb(nc.vector.tensor_copy, 1)
+        load_x_chunk(4)
         side_next = side_presort(0)
         t_waiting = []
 
         for s in range(32):
             u, zq, g = s // 16, (s % 16) // 4, s % 4
             load_emb(s + 3)
-            if s == 11:
+            if s == 2:
+                load_x_chunk(5)
+            if s == 20:
                 load_wp(0)
                 load_wp(1)
             if s == 16:
                 t_codes[1] = sbuf("t1_codes", [P, 4, 2048], U32, 1, OFF_B)
                 t_plane[1] = sbuf("t1_plane", [P, 2048], U8, 1, OFF_BP)
-            if s == 18:
+            if s == 21:
                 for n, vec in enumerate((bq, bk, bv)):
                     bt = sbuf("bias%d" % n, [P, 2048], BF16, 1, OFF_XS + n * 4 * KIB)
                     nc.sync.dma_start(out=bt[:], in_=vec.partition_broadcast(P))

@@ -39,6 +39,8 @@ OFF_PERM = 233 * KIB + 512
 OFF_CBB = 234 * KIB
 OFF_CBC = 234 * KIB + 64
 OFF_ST = 0
+OFF_WT = OFF_XRAW
+OFF_GW = OFF_XRAW + 8 * KIB
 
 
 def tile_swintransformerblock_pa_l_kernel(
@@ -56,7 +58,10 @@ def tile_swintransformerblock_pa_l_kernel(
         x_v = x.rearrange("b c (X i) (g w j) z -> (b c) i g X w (j z)", i=8, g=2, w=8, j=8)
         emb_v = emb_pos.rearrange("(X g w z) e -> g z X w e", X=16, g=2, w=8, z=16)
         wc_v = conv_w.rearrange("(g m t) c i j k -> g t m (c i j k)", g=4, t=4)
-        w_hbm = [Wq, Wk, Wv]
+        w_view = [
+            w.rearrange("o k -> (o k)").rearrange("(n a s q e) -> n q a s e", a=32, s=16, q=4, e=P)
+            for w in (Wq, Wk, Wv)
+        ]
         out_v = [
             o.rearrange("s r o -> (s r) o").rearrange(
                 "(gx gy gz m wz) o -> gy gz wz m gx o", gx=2, gy=2, gz=2, m=64, wz=8
@@ -152,37 +157,6 @@ def tile_swintransformerblock_pa_l_kernel(
 
         w_raw = {}
 
-        def load_w(key, rows):
-            wr = sbuf("wraw", [P, 2048], BF16, 2, OFF_WRAW)
-            nc.sync.dma_start(out=wr[:], in_=rows)
-            w_raw[key] = wr
-
-        def presort_w(copy, key):
-            ws = sbuf("ws", [P, 4, 2, P], F32, 3, OFF_WS)
-            copy(out=ws[:], in_=w_raw.pop(key)[:].bitcast(F32).rearrange("p (c m u) -> p c u m", c=4, u=2))
-            return ws
-
-        def w_banks(ws, codes, plane, col):
-            banks = []
-            for half in range(2):
-                banks.append(
-                    (
-                        [ws[:, 2 * half + a, v, :] for a in range(2) for v in range(2)],
-                        ident,
-                        None,
-                        [
-                            (
-                                512 * a,
-                                512 * (a + 1),
-                                codes[:, 2 * half + a, col : col + P],
-                                plane[4 * (2 * half + a) : P, col : col + P],
-                            )
-                            for a in range(2)
-                        ],
-                    )
-                )
-            return banks
-
         def load_wc(k):
             if k < 16:
                 wr = sbuf("wcraw", [P, 2048], BF16, 8, OFF_C)
@@ -217,7 +191,10 @@ def tile_swintransformerblock_pa_l_kernel(
 
         def load_wp(k):
             if k < 48:
-                load_w(("wp", k), w_hbm[k // 16][(k % 16) * P : (k % 16 + 1) * P, :])
+                wr = sbuf("wraw", [P, 16, P], BF16, 2, OFF_WRAW)
+                for q in range(4):
+                    nc.sync.dma_start(out=wr[32 * q : 32 * (q + 1), :, :], in_=w_view[k // 16][k % 16, q])
+                w_raw[("wp", k)] = wr
 
         er_tiles = {}
         es_tiles = {}
@@ -307,33 +284,72 @@ def tile_swintransformerblock_pa_l_kernel(
         wk_tiles = {}
         bias = []
 
-        def wp_presort(k):
-            ws = presort_w(nc.scalar.copy, ("wp", k))
-            load_wp(k + 2)
-            return ws
+        w_state = {}
 
-        def wp_banks(ws, k):
-            j, blk = divmod(k, 4)
-            if blk == 0:
-                wk_tiles[j] = (
-                    sbuf("wk", [P, 4, 512], U32, 2, OFF_WK),
-                    sbuf("wkp", [P, 512], U8, 2, OFF_WKP),
+        def wp_phase(k, phase):
+            if phase == 0:
+                ws = sbuf("ws", [P, 4, 2, P], F32, 3, OFF_WS)
+                src = (
+                    w_raw.pop(("wp", k))[:]
+                    .rearrange("p s e -> p (s e)")
+                    .bitcast(F32)
+                    .rearrange("p (r g b u) -> p u g r b", r=4, g=4, u=2)
                 )
-            return w_banks(ws, wk_tiles[j][0], wk_tiles[j][1], blk * P)
+                dst = ws[:].rearrange("p g u (r b) -> p u g r b", r=4)
+                for u in range(2):
+                    nc.scalar.copy(out=dst[:, u], in_=src[:, u])
+                load_wp(k + 2)
+                w_state[k] = ws
+            elif phase == 1:
+                wt = sbuf("wt", [P, 1024], F32, 2, OFF_WT)
+                nc.vector.transpose(out=wt[:], in_=w_state[k][:].rearrange("p g u c -> p (g u c)"))
+                w_state[k] = wt
+            elif phase == 2:
+                gw = sbuf("gw", [P, 2048], BF16, 2, OFF_GW)
+                nc.scalar.copy(
+                    out=gw[:].bitcast(F32).rearrange("p (g c u) -> p g c u", g=4, u=2),
+                    in_=w_state[k][:].rearrange("p (g u c) -> p g c u", g=4, u=2),
+                )
+                w_state[k] = gw
+            else:
+                j, blk = divmod(k, 4)
+                if blk == 0:
+                    wk_tiles[j] = (
+                        sbuf("wk", [P, 4, 512], U32, 2, OFF_WK),
+                        sbuf("wkp", [P, 512], U8, 2, OFF_WKP),
+                    )
+                quantize(
+                    w_state.pop(k),
+                    [
+                        (
+                            512 * g,
+                            512 * (g + 1),
+                            wk_tiles[j][0][:, g, blk * P : (blk + 1) * P],
+                            wk_tiles[j][1][4 * g : P, blk * P : (blk + 1) * P],
+                        )
+                        for g in range(4)
+                    ],
+                )
+
+        def wp_phases(table, when, phases):
+            for k, phase in table.get(when, []):
+                if phase in phases:
+                    wp_phase(k, phase)
+
+        s1_table = {}
+        for k in range(4):
+            for phase in range(4):
+                s1_table[19 + 3 * k + phase] = s1_table.get(19 + 3 * k + phase, []) + [(k, phase)]
 
         def side_presort(s):
             if 3 <= s < 19:
                 return presort_x(nc.scalar.copy, 4 + (s - 3) // 4, (s - 3) % 4)
-            if 24 <= s < 32:
-                return wp_presort(s - 24)
             return None
 
         def side_banks(s, thing):
             if thing is None:
                 return []
-            if s < 19:
-                return x_banks(thing, 4 + (s - 3) // 4, (s - 3) % 4)
-            return wp_banks(thing, s - 24)
+            return x_banks(thing, 4 + (s - 3) // 4, (s - 3) % 4)
 
         drain(2)
         load_x_chunk(4)
@@ -345,7 +361,7 @@ def tile_swintransformerblock_pa_l_kernel(
             load_emb(s + 3)
             if s == 2:
                 load_x_chunk(5)
-            if s == 20:
+            if s == 16:
                 load_wp(0)
                 load_wp(1)
             if s == 16:
@@ -375,6 +391,7 @@ def tile_swintransformerblock_pa_l_kernel(
                     run_banks(nc.scalar.copy, emb_banks(s + 1) + side_banks(s, side_next))
                     presort_emb(nc.scalar.copy, s + 2)
                     side_next = side_presort(s + 1)
+                    wp_phases(s1_table, s, (0, 2))
                 nc.vector.scalar_tensor_tensor(
                     out=tt[:, t, :],
                     in0=acc[:],
@@ -402,16 +419,17 @@ def tile_swintransformerblock_pa_l_kernel(
                 )
             )
             drain(2)
+            wp_phases(s1_table, s, (1, 3))
 
-        sorted_w = []
         for j in range(12):
             wsel, oc = divmod(j, 4)
-            prep = 4 * (j + 1) if 2 <= j + 1 < 12 else None
+            table = {}
+            if j + 1 < 12:
+                for n in range(4):
+                    for phase in range(4):
+                        table[1 + 7 * n + 2 * phase] = [(4 * (j + 1) + n, phase)]
             for tau in range(32):
                 u, Z = divmod(tau, 16)
-                if prep is not None and tau in (2, 14):
-                    first = prep + (0 if tau == 2 else 2)
-                    sorted_w = [(wp_presort(first), first), (wp_presort(first + 1), first + 1)]
                 acc = ps.tile([P, 512], F32, name="mm", tag="mm", bufs=4)
                 for G in range(4):
                     nc.tensor.matmul_mx(
@@ -423,17 +441,15 @@ def tile_swintransformerblock_pa_l_kernel(
                         start=(G == 0),
                         stop=(G == 3),
                     )
-                if prep is not None and tau in (6, 18):
-                    run_banks(
-                        nc.scalar.copy,
-                        wp_banks(sorted_w[0][0], sorted_w[0][1]) + wp_banks(sorted_w[1][0], sorted_w[1][1]),
-                    )
                 st = sbuf("st", [P, 512], F32, 12, OFF_ST)
                 nc.vector.tensor_tensor(
-                    out=st[:], in0=acc[:], in1=bias[wsel][:, oc * 512 : (oc + 1) * 512], op=ADD
+                    out=st[:].rearrange("p (k a r) -> p k a r", k=4, r=4),
+                    in0=acc[:].rearrange("p (k r a) -> p k a r", k=4, r=4),
+                    in1=bias[wsel][:, oc * 512 : (oc + 1) * 512].rearrange("p (k a r) -> p k a r", k=4, r=4),
+                    op=ADD,
                 )
                 nc.sync.dma_start(out=out_v[wsel][u, Z // 8, Z % 8, :, :, oc * 512 : (oc + 1) * 512], in_=st[:])
                 if len(t_waiting) > 0:
                     gt_old, specs_old = t_waiting.pop(0)
                     quantize(gt_old, specs_old)
-                drain(1)
+                wp_phases(table, tau, (0, 1, 2, 3))

@@ -285,6 +285,7 @@ def tile_swintransformerblock_pa_l_kernel(
         bias = []
 
         w_state = {}
+        w_turned = {}
 
         def wp_phase(k, phase):
             if phase == 0:
@@ -300,26 +301,31 @@ def tile_swintransformerblock_pa_l_kernel(
                     nc.scalar.copy(out=dst[:, u], in_=src[:, u])
                 load_wp(k + 2)
                 w_state[k] = ws
-            elif phase == 1:
-                wt = sbuf("wt", [P, 1024], F32, 2, OFF_WT)
-                nc.vector.transpose(out=wt[:], in_=w_state[k][:].rearrange("p g u c -> p (g u c)"))
-                w_state[k] = wt
-            elif phase == 2:
-                gw = sbuf("gw", [P, 2048], BF16, 2, OFF_GW)
-                nc.scalar.copy(
-                    out=gw[:].bitcast(F32).rearrange("p (g c u) -> p g c u", g=4, u=2),
-                    in_=w_state[k][:].rearrange("p (g u c) -> p g c u", g=4, u=2),
+            elif phase <= 4:
+                g = phase - 1
+                if g == 0:
+                    w_turned[k] = sbuf("wt", [P, 4, 256], F32, 2, OFF_WT)
+                nc.vector.transpose(
+                    out=w_turned[k][:, g, :], in_=w_state[k][:, g, :, :].rearrange("p u c -> p (u c)")
                 )
+            elif phase == 5:
+                gw = sbuf("gw", [P, 2048], BF16, 2, OFF_GW)
+                wt = w_turned.pop(k)
+                for g in range(4):
+                    nc.scalar.copy(
+                        out=gw[:].bitcast(F32).rearrange("p (g a r u) -> p g a r u", g=4, r=4, u=2)[:, g],
+                        in_=wt[:, g, :].rearrange("p (u r a) -> p a r u", u=2, r=4),
+                    )
                 w_state[k] = gw
             else:
                 j, blk = divmod(k, 4)
-                if blk == 0:
+                if blk == 0 and phase == 6:
                     wk_tiles[j] = (
                         sbuf("wk", [P, 4, 512], U32, 2, OFF_WK),
                         sbuf("wkp", [P, 512], U8, 2, OFF_WKP),
                     )
                 quantize(
-                    w_state.pop(k),
+                    w_state[k],
                     [
                         (
                             512 * g,
@@ -327,7 +333,7 @@ def tile_swintransformerblock_pa_l_kernel(
                             wk_tiles[j][0][:, g, blk * P : (blk + 1) * P],
                             wk_tiles[j][1][4 * g : P, blk * P : (blk + 1) * P],
                         )
-                        for g in range(4)
+                        for g in (2 * (phase - 6), 2 * (phase - 6) + 1)
                     ],
                 )
 
@@ -338,8 +344,8 @@ def tile_swintransformerblock_pa_l_kernel(
 
         s1_table = {}
         for k in range(4):
-            for phase in range(4):
-                s1_table[19 + 3 * k + phase] = s1_table.get(19 + 3 * k + phase, []) + [(k, phase)]
+            for phase, late in enumerate((0, 1, 1, 1, 1, 2, 3, 3)):
+                s1_table[18 + 3 * k + late] = s1_table.get(18 + 3 * k + late, []) + [(k, phase)]
 
         def side_presort(s):
             if 3 <= s < 19:
@@ -361,7 +367,7 @@ def tile_swintransformerblock_pa_l_kernel(
             load_emb(s + 3)
             if s == 2:
                 load_x_chunk(5)
-            if s == 16:
+            if s == 13:
                 load_wp(0)
                 load_wp(1)
             if s == 16:
@@ -391,7 +397,7 @@ def tile_swintransformerblock_pa_l_kernel(
                     run_banks(nc.scalar.copy, emb_banks(s + 1) + side_banks(s, side_next))
                     presort_emb(nc.scalar.copy, s + 2)
                     side_next = side_presort(s + 1)
-                    wp_phases(s1_table, s, (0, 2))
+                    wp_phases(s1_table, s, (0, 5))
                 nc.vector.scalar_tensor_tensor(
                     out=tt[:, t, :],
                     in0=acc[:],
@@ -419,18 +425,21 @@ def tile_swintransformerblock_pa_l_kernel(
                 )
             )
             drain(2)
-            wp_phases(s1_table, s, (1, 3))
+            wp_phases(s1_table, s, (1, 2, 3, 4, 6, 7))
 
         for j in range(12):
             wsel, oc = divmod(j, 4)
             table = {}
             if j + 1 < 12:
                 for n in range(4):
-                    for phase in range(4):
-                        table[1 + 7 * n + 2 * phase] = [(4 * (j + 1) + n, phase)]
+                    for phase in range(8):
+                        table[6 * n + phase] = table.get(6 * n + phase, []) + [(4 * (j + 1) + n, phase)]
             for tau in range(32):
                 u, Z = divmod(tau, 16)
-                acc = ps.tile([P, 512], F32, name="mm", tag="mm", bufs=4)
+                if tau % 2 == 0:
+                    acc = ps.tile([P, 512], F32, name="mm", tag="mm", bufs=4)
+                else:
+                    acc = ps.tile([P, 512], F32, name="tp", tag="tp", bufs=4)
                 for G in range(4):
                     nc.tensor.matmul_mx(
                         out=acc[:],
@@ -441,15 +450,12 @@ def tile_swintransformerblock_pa_l_kernel(
                         start=(G == 0),
                         stop=(G == 3),
                     )
-                st = sbuf("st", [P, 512], F32, 12, OFF_ST)
+                st = sbuf("st", [P, 512], F32, 16, OFF_ST)
                 nc.vector.tensor_tensor(
-                    out=st[:].rearrange("p (k a r) -> p k a r", k=4, r=4),
-                    in0=acc[:].rearrange("p (k r a) -> p k a r", k=4, r=4),
-                    in1=bias[wsel][:, oc * 512 : (oc + 1) * 512].rearrange("p (k a r) -> p k a r", k=4, r=4),
-                    op=ADD,
+                    out=st[:], in0=acc[:], in1=bias[wsel][:, oc * 512 : (oc + 1) * 512], op=ADD
                 )
                 nc.sync.dma_start(out=out_v[wsel][u, Z // 8, Z % 8, :, :, oc * 512 : (oc + 1) * 512], in_=st[:])
                 if len(t_waiting) > 0:
                     gt_old, specs_old = t_waiting.pop(0)
                     quantize(gt_old, specs_old)
-                wp_phases(table, tau, (0, 1, 2, 3))
+                wp_phases(table, tau, (0, 1, 2, 3, 4, 5, 6, 7))

from contextlib import ExitStack

import concourse.mybir as mybir
from concourse.masks import make_identity

FLOPS = 4 * 2 * 4096 * 2048 * 2048

F32 = mybir.dt.float32
BF16 = mybir.dt.bfloat16
U32 = mybir.dt.uint32
U8 = mybir.dt.uint8
FP8X4 = mybir.dt.float8_e4m3fn_x4
ADD = mybir.AluOpType.add

P = 128
KIB = 1024

OFF_WC = 0
OFF_WCP = 32 * KIB
OFF_B = 34 * KIB
OFF_BP = 66 * KIB
OFF_C = 68 * KIB
OFF_CP = 100 * KIB
OFF_D = 102 * KIB
OFF_DP = 134 * KIB
OFF_XRAW = 136 * KIB
OFF_WK = 152 * KIB
OFF_WKP = 168 * KIB
OFF_XS = 169 * KIB
OFF_WRAW = 181 * KIB
OFF_WS = 189 * KIB
OFF_GRP = 201 * KIB
OFF_ER = 209 * KIB
OFF_EMBT = 217 * KIB
OFF_TT = 225 * KIB
OFF_GT = 229 * KIB
OFF_ID = 233 * KIB
OFF_PERM = 233 * KIB + 512
OFF_CBB = 234 * KIB
OFF_CBC = 234 * KIB + 64
OFF_ST = 0
OFF_WT = OFF_XRAW
OFF_GW = OFF_XRAW + 8 * KIB


def tile_swintransformerblock_pa_l_kernel(
    tc, x, conv_w, conv_b, emb_pos, Wq, bq, Wk, bk, Wv, bv, out_0, out_1, out_2
):
    nc = tc.nc
    with ExitStack() as ctx:
        sb = ctx.enter_context(tc.tile_pool(name="sb", bufs=1))
        ps = ctx.enter_context(tc.psum_pool(name="ps", bufs=4))
        ctx.enter_context(tc.manual_schedule())

        def sbuf(tag, shape, dtype, bufs, offset):
            return sb.tile(shape, dtype, name=tag, tag=tag, bufs=bufs, offset=offset, align_bytes=64)

        x_v = x.rearrange("b c (X i) (g w j) z -> (b c) i g X w (j z)", i=8, g=2, w=8, j=8)
        emb_v = emb_pos.rearrange("(X g w z) e -> g z X w e", X=16, g=2, w=8, z=16)
        wc_v = conv_w.rearrange("(g m t) c i j k -> g t m (c i j k)", g=4, t=4)
        w_view = [
            w.rearrange("o k -> (o k)").rearrange("(n a s q e) -> n q a s e", a=32, s=16, q=4, e=P)
            for w in (Wq, Wk, Wv)
        ]
        out_v = [
            o.rearrange("s r o -> (s r) o").rearrange(
                "(gx gy gz m wz) o -> gy gz wz m gx o", gx=2, gy=2, gz=2, m=64, wz=8
            )
            for o in (out_0, out_1, out_2)
        ]

        ident = sbuf("ident", [P, P], F32, 1, OFF_ID)
        make_identity(nc, ident[:])
        perm = sbuf("perm", [P, P], F32, 1, OFF_PERM)
        nc.vector.tensor_copy(
            out=perm[:].rearrange("p (m g) -> p g m", g=2), in_=ident[:].rearrange("p (g m) -> p g m", g=2)
        )

        wc_codes = sbuf("wc_codes", [P, 4, 2048], U32, 1, OFF_WC)
        wc_plane = sbuf("wc_plane", [P, 2048], U8, 1, OFF_WCP)
        x_codes = [sbuf("x0_codes", [P, 4, 2048], U32, 1, OFF_B), None]
        x_plane = [sbuf("x0_plane", [P, 2048], U8, 1, OFF_BP), None]

        pending = []

        def quantize(grp, specs):
            for lo, hi, codes, plane in specs:
                nc.vector.quantize_mx(out=codes.bitcast(FP8X4), scales=plane, in_=grp[:, lo:hi])

        def drain(count):
            for n in range(min(count, len(pending))):
                grp, specs = pending.pop(0)
                quantize(grp, specs)

        def run_banks(copy, banks):
            tps = []
            for sources, matrix, dest, specs in banks:
                tp = ps.tile([P, 512], F32, name="tp", tag="tp", bufs=4)
                for n, src in enumerate(sources):
                    nc.tensor.transpose(tp[:, n * P : (n + 1) * P], src, matrix[:])
                tps.append(tp)
            for tp, bank in zip(tps, banks):
                if bank[2] is not None:
                    copy(out=bank[2], in_=tp[:])
                else:
                    grp = sbuf("grp", [P, 1024], BF16, 4, OFF_GRP)
                    copy(
                        out=grp[:].bitcast(F32).rearrange("p (a r u) -> p a r u", a=2, u=2),
                        in_=tp[:].rearrange("p (a u r) -> p a r u", a=2, u=2),
                    )
                    pending.append((grp, bank[3]))

        x_raw = {}

        def load_x_chunk(ci):
            if ci >= 8:
                return
            u, c = divmod(ci, 4)
            if ci in (2, 3):
                xr = sbuf("xrawd", [P, 8, 1024], BF16, 2, OFF_D)
            else:
                xr = sbuf("xraw", [P, 8, 1024], BF16, 2, OFF_XRAW)
            for i in range(8):
                nc.sync.dma_start(out=xr[:, i, :], in_=x_v[c, i, u])
            x_raw[ci] = xr

        def presort_x(copy, ci, zq):
            xs = sbuf("xs", [P, 4, 2, P], F32, 3, OFF_XS)
            src = (
                x_raw[ci][:]
                .rearrange("p i e -> p (i e)")
                .bitcast(F32)
                .rearrange("p (a z k u) -> p u z a k", a=64, z=16, k=2, u=2)
            )
            dst = xs[:].rearrange("p z u (a k) -> p u z a k", k=2)
            for u in range(2):
                copy(out=dst[:, u], in_=src[:, u, 4 * zq : 4 * zq + 4])
            if zq == 3 and ci >= 4:
                load_x_chunk(ci + 2)
            return xs

        def x_banks(xs, ci, zq):
            u, c = divmod(ci, 4)
            banks = []
            for half in range(2):
                z0 = 4 * zq + 2 * half
                cols = (z0 * P, (z0 + 2) * P)
                banks.append(
                    (
                        [xs[:, 2 * half + a, v, :] for a in range(2) for v in range(2)],
                        perm,
                        None,
                        [(0, 1024, x_codes[u][:, c, cols[0] : cols[1]], x_plane[u][4 * c : P, cols[0] : cols[1]])],
                    )
                )
            return banks

        w_raw = {}

        def load_wc(k):
            if k < 16:
                wr = sbuf("wcraw", [P, 2048], BF16, 8, OFF_C)
                nc.sync.dma_start(out=wr[:], in_=wc_v[k // 4, k % 4])
                w_raw[("wc", k)] = wr

        def wc_banks(k):
            words = w_raw.pop(("wc", k))[:].bitcast(F32)
            banks = []
            for half in range(2):
                banks.append(
                    (
                        [
                            words[:, 256 * (2 * half + a) + v : 256 * (2 * half + a + 1) : 2]
                            for a in range(2)
                            for v in range(2)
                        ],
                        ident,
                        None,
                        [
                            (
                                512 * a,
                                512 * (a + 1),
                                wc_codes[:, 2 * half + a, k * P : (k + 1) * P],
                                wc_plane[4 * (2 * half + a) : P, k * P : (k + 1) * P],
                            )
                            for a in range(2)
                        ],
                    )
                )
            return banks

        def load_wp(k):
            if k < 48:
                wr = sbuf("wraw", [P, 16, P], BF16, 2, OFF_WRAW)
                for q in range(4):
                    nc.sync.dma_start(out=wr[32 * q : 32 * (q + 1), :, :], in_=w_view[k // 16][k % 16, q])
                w_raw[("wp", k)] = wr

        er_tiles = {}
        es_tiles = {}
        emb_t = {}

        def load_emb(s):
            if s >= 32:
                return
            er = sbuf("er", [P, 4, 512], BF16, 2, OFF_ER)
            for z in range(4):
                nc.sync.dma_start(
                    out=er[:, z, :],
                    in_=emb_v[s // 16, 4 * ((s % 16) // 4) + z, :, :, (s % 4) * 512 : (s % 4 + 1) * 512],
                )
            er_tiles[s] = er

        def presort_emb(copy, s):
            if s >= 32:
                return
            es = sbuf("ws", [P, 4, 2, P], F32, 3, OFF_WS)
            copy(
                out=es[:],
                in_=er_tiles.pop(s)[:]
                .rearrange("p z e -> p (z e)")
                .bitcast(F32)
                .rearrange("p (z m v) -> p z v m", z=4, v=2),
            )
            es_tiles[s] = es

        def emb_banks(s):
            if s >= 32:
                return []
            es = es_tiles.pop(s)
            et = sbuf("embt", [P, 2, 512], F32, 2, OFF_EMBT)
            emb_t[s] = et
            return [([es[:, z, v, :] for z in range(4)], perm, et[:, v, :], None) for v in range(2)]

        cbb = sbuf("cbb", [P, 4, 4], BF16, 1, OFF_CBB)
        nc.sync.dma_start(out=cbb[:], in_=conv_b.rearrange("(g p t) -> p g t", g=4, t=4))
        load_x_chunk(0)
        for k in range(4):
            load_wc(k)
        load_x_chunk(1)
        for k in range(4, 8):
            load_wc(k)
        load_x_chunk(2)

        def head_presort(n):
            if n % 2 == 0:
                return presort_x(nc.vector.tensor_copy, n // 8, (n % 8) // 2)
            return None

        cbc = sbuf("cbc", [P, 16], F32, 1, OFF_CBC)
        sorted_next = head_presort(0)
        for n in range(32):
            sorted_now = sorted_next
            if n + 1 < 32:
                sorted_next = head_presort(n + 1)
            if n % 2 == 0:
                banks = x_banks(sorted_now, n // 8, (n % 8) // 2)
            else:
                banks = wc_banks(n // 2)
            run_banks(nc.scalar.copy, banks)
            if n % 2 == 1:
                load_wc(n // 2 + 8)
            if n == 7:
                load_x_chunk(3)
            if n == 9:
                load_emb(0)
                load_emb(1)
            if n == 20:
                nc.vector.tensor_copy(out=cbc[:], in_=cbb[:].rearrange("p g t -> p (g t)"))
            if n == 27:
                presort_emb(nc.vector.tensor_copy, 0)
                load_emb(2)
            if n == 29:
                run_banks(nc.scalar.copy, emb_banks(0))
            if n == 30:
                presort_emb(nc.vector.tensor_copy, 1)
            if n > 0:
                drain(2)

        x_codes[1] = sbuf("x1_codes", [P, 4, 2048], U32, 1, OFF_C)
        x_plane[1] = sbuf("x1_plane", [P, 2048], U8, 1, OFF_CP)
        t_codes = [sbuf("t0_codes", [P, 4, 2048], U32, 1, OFF_D), None]
        t_plane = [sbuf("t0_plane", [P, 2048], U8, 1, OFF_DP), None]
        wk_tiles = {}
        bias = []

        w_state = {}
        w_turned = {}

        def wp_phase(k, phase):
            if phase == 0:
                ws = sbuf("ws", [P, 4, 2, P], F32, 3, OFF_WS)
                src = (
                    w_raw.pop(("wp", k))[:]
                    .rearrange("p s e -> p (s e)")
                    .bitcast(F32)
                    .rearrange("p (r g b u) -> p u g r b", r=4, g=4, u=2)
                )
                dst = ws[:].rearrange("p g u (r b) -> p u g r b", r=4)
                for u in range(2):
                    nc.scalar.copy(out=dst[:, u], in_=src[:, u])
                load_wp(k + 2)
                w_state[k] = ws
            elif phase <= 4:
                g = phase - 1
                if g == 0:
                    w_turned[k] = sbuf("wt", [P, 4, 256], F32, 2, OFF_WT)
                nc.vector.transpose(
                    out=w_turned[k][:, g, :], in_=w_state[k][:, g, :, :].rearrange("p u c -> p (u c)")
                )
            elif phase == 5:
                gw = sbuf("gw", [P, 2048], BF16, 2, OFF_GW)
                wt = w_turned.pop(k)
                for g in range(4):
                    nc.scalar.copy(
                        out=gw[:].bitcast(F32).rearrange("p (g a r u) -> p g a r u", g=4, r=4, u=2)[:, g],
                        in_=wt[:, g, :].rearrange("p (u r a) -> p a r u", u=2, r=4),
                    )
                w_state[k] = gw
            else:
                j, blk = divmod(k, 4)
                if blk == 0 and phase == 6:
                    wk_tiles[j] = (
                        sbuf("wk", [P, 4, 512], U32, 2, OFF_WK),
                        sbuf("wkp", [P, 512], U8, 2, OFF_WKP),
                    )
                quantize(
                    w_state[k],
                    [
                        (
                            512 * g,
                            512 * (g + 1),
                            wk_tiles[j][0][:, g, blk * P : (blk + 1) * P],
                            wk_tiles[j][1][4 * g : P, blk * P : (blk + 1) * P],
                        )
                        for g in (2 * (phase - 6), 2 * (phase - 6) + 1)
                    ],
                )

        def wp_phases(table, when, phases):
            for k, phase in table.get(when, []):
                if phase in phases:
                    wp_phase(k, phase)

        s1_table = {}
        for k in range(4):
            for phase, late in enumerate((0, 1, 1, 1, 1, 2, 3, 3)):
                s1_table[18 + 3 * k + late] = s1_table.get(18 + 3 * k + late, []) + [(k, phase)]

        def side_presort(s):
            if 3 <= s < 19:
                return presort_x(nc.scalar.copy, 4 + (s - 3) // 4, (s - 3) % 4)
            return None

        def side_banks(s, thing):
            if thing is None:
                return []
            return x_banks(thing, 4 + (s - 3) // 4, (s - 3) % 4)

        drain(2)
        load_x_chunk(4)
        side_next = side_presort(0)
        t_waiting = []

        for s in range(32):
            u, zq, g = s // 16, (s % 16) // 4, s % 4
            load_emb(s + 3)
            if s == 2:
                load_x_chunk(5)
            if s == 13:
                load_wp(0)
                load_wp(1)
            if s == 16:
                t_codes[1] = sbuf("t1_codes", [P, 4, 2048], U32, 1, OFF_B)
                t_plane[1] = sbuf("t1_plane", [P, 2048], U8, 1, OFF_BP)
            if s == 21:
                for n, vec in enumerate((bq, bk, bv)):
                    bt = sbuf("bias%d" % n, [P, 2048], BF16, 1, OFF_XS + n * 4 * KIB)
                    nc.sync.dma_start(out=bt[:], in_=vec.partition_broadcast(P))
                    bias.append(bt)
            tt = sbuf("tt", [P, 4, 512], BF16, 1, OFF_TT)
            et = emb_t.pop(s)
            for t in range(4):
                col = (4 * g + t) * P
                acc = ps.tile([P, 512], F32, name="mm", tag="mm", bufs=4)
                for c in range(4):
                    nc.tensor.matmul_mx(
                        out=acc[:],
                        lhsT=wc_codes[:, c, col : col + P].bitcast(FP8X4),
                        lhsT_scale=wc_plane[4 * c : P, col : col + P],
                        rhs=x_codes[u][:, c, zq * 512 : (zq + 1) * 512].bitcast(FP8X4),
                        rhs_scale=x_plane[u][4 * c : P, zq * 512 : (zq + 1) * 512],
                        start=(c == 0),
                        stop=(c == 3),
                    )
                if t == 1:
                    run_banks(nc.scalar.copy, emb_banks(s + 1) + side_banks(s, side_next))
                    presort_emb(nc.scalar.copy, s + 2)
                    side_next = side_presort(s + 1)
                    wp_phases(s1_table, s, (0, 5))
                nc.vector.scalar_tensor_tensor(
                    out=tt[:, t, :],
                    in0=acc[:],
                    scalar=cbc[:, 4 * g + t : 4 * g + t + 1],
                    in1=et[:, t // 2, :].bitcast(BF16).rearrange("p (n h) -> p n h", h=2)[:, :, t % 2],
                    op0=ADD,
                    op1=ADD,
                )
                if t == 0 and len(t_waiting) > 0:
                    gt_old, specs_old = t_waiting.pop(0)
                    quantize(gt_old, specs_old)
            gt = sbuf("gt", [P, 2048], BF16, 1, OFF_GT)
            nc.vector.tensor_copy(out=gt[:].rearrange("p (n t) -> p n t", t=4), in_=tt[:].rearrange("p t n -> p n t"))
            t_waiting.append(
                (
                    gt,
                    [
                        (
                            0,
                            2048,
                            t_codes[u][:, g, zq * 512 : (zq + 1) * 512],
                            t_plane[u][4 * g : P, zq * 512 : (zq + 1) * 512],
                        )
                    ],
                )
            )
            drain(2)
            wp_phases(s1_table, s, (1, 2, 3, 4, 6, 7))

        for j in range(12):
            wsel, oc = divmod(j, 4)
            table = {}
            if j + 1 < 12:
                for n in range(4):
                    for phase in range(8):
                        table[6 * n + phase] = table.get(6 * n + phase, []) + [(4 * (j + 1) + n, phase)]
            for tau in range(32):
                u, Z = divmod(tau, 16)
                if tau % 2 == 0:
                    acc = ps.tile([P, 512], F32, name="mm", tag="mm", bufs=4)
                else:
                    acc = ps.tile([P, 512], F32, name="tp", tag="tp", bufs=4)
                for G in range(4):
                    nc.tensor.matmul_mx(
                        out=acc[:],
                        lhsT=t_codes[u][:, G, Z * P : (Z + 1) * P].bitcast(FP8X4),
                        lhsT_scale=t_plane[u][4 * G : P, Z * P : (Z + 1) * P],
                        rhs=wk_tiles[j][0][:, G, :].bitcast(FP8X4),
                        rhs_scale=wk_tiles[j][1][4 * G : P, :],
                        start=(G == 0),
                        stop=(G == 3),
                    )
                st = sbuf("st", [P, 512], F32, 16, OFF_ST)
                nc.vector.tensor_tensor(
                    out=st[:], in0=acc[:], in1=bias[wsel][:, oc * 512 : (oc + 1) * 512], op=ADD
                )
                nc.sync.dma_start(out=out_v[wsel][u, Z // 8, Z % 8, :, :, oc * 512 : (oc + 1) * 512], in_=st[:])
                if len(t_waiting) > 0:
                    gt_old, specs_old = t_waiting.pop(0)
                    quantize(gt_old, specs_old)
                wp_phases(table, tau, (0, 1, 2, 3, 4, 5, 6, 7))
